import numpy as np
import ml_dtypes


def mxq(x, axis, fmt="e4m3"):
    dtype, down = {"e4m3": (ml_dtypes.float8_e4m3fn, 7), "e5m2": (ml_dtypes.float8_e5m2, 14)}[fmt]
    v = np.moveaxis(np.asarray(x, np.float32).astype(ml_dtypes.bfloat16).astype(np.float64), axis, -1)
    blocks = v.reshape(v.shape[:-1] + (-1, 32))
    amax = np.abs(blocks).max(-1, keepdims=True)
    byte = np.maximum(np.where(amax > 0, np.frexp(amax)[1] - 1 + 127, 0) - down, 1)
    scale = np.exp2(byte - 127.0)
    codes = (blocks / scale).astype(np.float32).astype(dtype).astype(np.float64)
    return np.moveaxis((codes * scale).reshape(v.shape), -1, axis)


WIDE = False


def mx_kscale(k):
    if not WIDE:
        return np.ones(k)
    levels = np.array([10, -10, 5, -5, 0])
    if k % 512:
        return np.exp2(np.random.permutation(np.resize(levels, k // 32))).repeat(32)
    a = np.empty((k // 512, 16))
    for p in range(k // 512):
        a[p, :8] = np.random.permutation(np.resize(levels, 8))
        for g in range(8):
            far = levels[np.abs(levels - a[p, g]) >= 10]
            a[p, g + 8] = far[np.random.randint(len(far))]
    return np.exp2(a.ravel()).repeat(32)


BF16 = ml_dtypes.bfloat16


def bf(x):
    return np.asarray(x, np.float32).astype(BF16)


def f64(x):
    return np.asarray(x).astype(np.float64)


B, D, C, NP, NS = 4096, 1024, 512, 512, 512


def relu(v):
    return np.maximum(v, 0.0)


def setup_inputs():
    s = mx_kscale(D)
    t = mx_kscale(NS)
    return {
        "x_batch": bf(np.random.uniform(size=(B, D)) * s),
        "predicted": bf(np.random.standard_normal((B, D)) * s),
        "W_vip_td": bf(np.random.standard_normal((NS, D)) / np.sqrt(D) / s * t[:, None]),
        "W_som_in": bf(np.random.standard_normal((NS, D)) * 1.5 / np.sqrt(D) / s),
        "W_vip_som": bf(np.random.standard_normal((NS, NS)) / np.sqrt(NS) / t),
    }


def reference(x_batch, predicted, W_vip_td, W_som_in, W_vip_som):
    r_vip = relu(mxq(f64(predicted), 1, "e4m3") @ mxq(f64(W_vip_td), 1, "e4m3").T)
    som_ff = relu(mxq(f64(x_batch), 1, "e4m3") @ mxq(f64(W_som_in), 1, "e4m3").T)
    r_som = relu(som_ff - (mxq(r_vip, 1, "e4m3") @ mxq(f64(W_vip_som), 1, "e4m3").T))
    return r_som

@@ -1,0 +1,286 @@
+from contextlib import ExitStack
+
+import concourse.mybir as mybir
+from concourse.masks import make_identity
+
+F32 = mybir.dt.float32
+BF16 = mybir.dt.bfloat16
+U32 = mybir.dt.uint32
+U8 = mybir.dt.uint8
+FP8X4 = mybir.dt.float8_e4m3fn_x4
+RELU = mybir.ActivationFunctionType.Relu
+SUBTRACT = mybir.AluOpType.subtract
+MIN = mybir.AluOpType.min
+MAX = mybir.AluOpType.max
+
+BATCH = 4096
+D_IN = 1024
+CELLS = 512
+FLOPS = 2 * BATCH * CELLS * (2 * D_IN + CELLS)
+
+P = 128
+PACK = 4
+K_PASS = P * PACK
+D_PASSES = D_IN // K_PASS
+BANK = 512
+BLOCKS = BANK // P
+
+TILES = BATCH // P
+CHUNK_TILES = 2
+CHUNKS = TILES // CHUNK_TILES
+ROUND_CHUNKS = 2
+ROUND_TILES = ROUND_CHUNKS * CHUNK_TILES
+UNITS = CHUNKS // ROUND_CHUNKS
+X_LAG = 1
+LOAD_AHEAD = 2
+VECTOR_SHARE = 2
+
+
+def tile_pecircuits_pa_t_kernel(
+    tc, x_batch, predicted, W_vip_td, W_som_in, W_vip_som, out
+):
+    nc = tc.nc
+
+    pred_chunks = predicted.rearrange("(c p t) k -> c p (t k)", p=P, t=CHUNK_TILES)
+    x_chunks = x_batch.rearrange("(c p t) k -> c p (t k)", p=P, t=CHUNK_TILES)
+    out_chunks = out.rearrange("(c p t) n -> c p (t n)", p=P, t=CHUNK_TILES)
+
+    with ExitStack() as stack:
+        const = stack.enter_context(tc.tile_pool(name="const", bufs=1))
+        raw_pool = stack.enter_context(
+            tc.tile_pool(name="raw", bufs=(LOAD_AHEAD + 1) * ROUND_CHUNKS)
+        )
+        grouped_pool = stack.enter_context(tc.tile_pool(name="grouped", bufs=3 * ROUND_TILES))
+        codes_pool = stack.enter_context(tc.tile_pool(name="codes", bufs=3 * ROUND_TILES))
+        vip_pool = stack.enter_context(
+            tc.tile_pool(name="vip", bufs=(X_LAG + 3) * ROUND_TILES)
+        )
+        som_pool = stack.enter_context(tc.tile_pool(name="som", bufs=4))
+        out_pool = stack.enter_context(tc.tile_pool(name="result", bufs=6))
+        psum = stack.enter_context(tc.psum_pool(name="psum", bufs=8))
+        stack.enter_context(tc.manual_schedule())
+
+        ident = const.tile([P, P], F32)
+        make_identity(nc, ident[:])
+
+        def as_pairs(words):
+            return words.rearrange("p (g b u) -> p g b u", g=D_PASSES, u=2)
+
+        def flip(words, dest, copy_out):
+            bank = psum.tile([P, BANK], F32, tag="bank")
+            for c in range(BLOCKS):
+                g, u = divmod(c, 2)
+                nc.tensor.transpose(
+                    bank[:, c * P : (c + 1) * P],
+                    words[:, 2 * g * P + u : 2 * (g + 1) * P : 2],
+                    ident[:],
+                )
+            copy_out(out=dest, in_=bank[:].rearrange("p (g u b) -> p g b u", g=D_PASSES, u=2))
+
+        def quantise(grouped, codes, scales):
+            nc.vector.quantize_mx(out=codes.bitcast(FP8X4), scales=scales, in_=grouped)
+
+        def mx(acc, stationary, s_cols, moving, m_cols, start, stop):
+            nc.tensor.matmul_mx(
+                out=acc,
+                lhsT=stationary[0][:, s_cols].bitcast(FP8X4),
+                lhsT_scale=stationary[1][:, s_cols],
+                rhs=moving[0][:, m_cols].bitcast(FP8X4),
+                rhs_scale=moving[1][:, m_cols],
+                start=start,
+                stop=stop,
+            )
+
+        td_raw = const.tile([P, PACK * D_IN], BF16)
+        td_q = (
+            const.tile([P, PACK * D_PASSES * P], U32, name="td_codes", align_bytes=64),
+            const.tile([P, PACK * D_PASSES * P], U8, name="td_scales", align_bytes=64),
+        )
+        som_raw = const.tile([P, BLOCKS * D_IN], BF16)
+        som_grouped = const.tile([P, D_PASSES * CELLS * PACK], BF16, align_bytes=64)
+        som_q = (
+            const.tile([P, D_PASSES * CELLS], U32, name="som_codes", align_bytes=64),
+            const.tile([P, D_PASSES * CELLS], U8, name="som_scales", align_bytes=64),
+        )
+        vs_raw = const.tile([P, BLOCKS * CELLS], BF16)
+        vs_grouped = const.tile([P, CELLS * PACK], BF16, align_bytes=64)
+        vs_q = (
+            const.tile([P, CELLS], U32, name="vs_codes", align_bytes=64),
+            const.tile([P, CELLS], U8, name="vs_scales", align_bytes=64),
+        )
+
+        def either_copy(n):
+            return nc.scalar.copy if n % 2 == 0 else nc.vector.tensor_copy
+
+        def load_td():
+            rows = W_vip_td.rearrange("(q j) k -> q (j k)", j=PACK)
+            for u in range(2):
+                half = slice(u * 2 * D_IN, (u + 1) * 2 * D_IN)
+                nc.sync.dma_start(out=td_raw[:, half], in_=rows[:, half])
+
+        def prepare_td():
+            tiles = []
+            for j in range(PACK):
+                grouped = grouped_pool.tile([P, 2 * BANK], BF16, tag="grouped", align_bytes=64)
+                flip(
+                    td_raw[:].bitcast(F32)[:, j * BANK : (j + 1) * BANK],
+                    as_pairs(grouped[:].bitcast(F32)),
+                    either_copy(j),
+                )
+                tiles.append(grouped)
+            for j in range(PACK):
+                cols = slice(j * D_PASSES * P, (j + 1) * D_PASSES * P)
+                quantise(tiles[j][:], td_q[0][:, cols], td_q[1][:, cols])
+
+        def load_som_and_vs():
+            nc.sync.dma_start(
+                out=som_raw[:].rearrange("q (r k) -> q r k", r=BLOCKS),
+                in_=W_som_in.rearrange("(r q) k -> q r k", q=P),
+            )
+            nc.sync.dma_start(
+                out=vs_raw[:].rearrange("q (r k) -> q r k", r=BLOCKS),
+                in_=W_vip_som.rearrange("(r q) k -> q r k", q=P),
+            )
+
+        def prepare_som_and_vs():
+            som_words = som_grouped[:].bitcast(F32).rearrange(
+                "p (g r q u) -> p r g q u", g=D_PASSES, r=BLOCKS, u=2
+            )
+            for r in range(BLOCKS):
+                flip(
+                    som_raw[:].bitcast(F32)[:, r * BANK : (r + 1) * BANK],
+                    som_words[:, r],
+                    either_copy(r),
+                )
+            for h in range(2):
+                half = slice(h * BANK, (h + 1) * BANK)
+                flip(
+                    vs_raw[:].bitcast(F32)[:, half],
+                    as_pairs(vs_grouped[:].bitcast(F32)[:, half]),
+                    either_copy(h),
+                )
+            quantise(som_grouped[:], som_q[0][:], som_q[1][:])
+            quantise(vs_grouped[:], vs_q[0][:], vs_q[1][:])
+
+        raw = {}
+        grouped_of = {}
+        quantised = {}
+
+        def chunks_of(unit):
+            if 0 <= unit < UNITS:
+                return range(unit * ROUND_CHUNKS, (unit + 1) * ROUND_CHUNKS)
+            return range(0)
+
+        def tiles_of(unit):
+            return [c * CHUNK_TILES + t for c in chunks_of(unit) for t in range(CHUNK_TILES)]
+
+        def load(name, chunks, c):
+            rows = raw_pool.tile([P, CHUNK_TILES * D_IN], BF16, tag=name + "_raw")
+            nc.sync.dma_start(out=rows[:], in_=chunks[c])
+            raw[(name, c)] = rows
+
+        def loads_for_round(r):
+            if r == X_LAG + 1:
+                load_som_and_vs()
+            for c in chunks_of(r):
+                load("pred", pred_chunks, c)
+            for c in chunks_of(r - 1 - X_LAG):
+                load("x", x_chunks, c)
+
+        def flip_tile(name, i, copy_out):
+            c, t = divmod(i, CHUNK_TILES)
+            grouped = grouped_pool.tile([P, 2 * BANK], BF16, tag="grouped", align_bytes=64)
+            flip(
+                raw[(name, c)][:].bitcast(F32)[:, t * BANK : (t + 1) * BANK],
+                as_pairs(grouped[:].bitcast(F32)),
+                copy_out,
+            )
+            grouped_of[(name, i)] = grouped
+
+        def quantise_tile(name, i, pool):
+            grouped = grouped_of[(name, i)]
+            width = grouped.shape[1] // PACK
+            codes = pool.tile([P, width], U32, tag=name + "_codes", align_bytes=64)
+            scales = pool.tile([P, width], U8, tag=name + "_scales", align_bytes=64)
+            quantise(grouped[:], codes[:], scales[:])
+            quantised[(name, i)] = (codes, scales)
+
+        def vip_matmul(i):
+            bank = psum.tile([P, BANK], F32, tag="bank")
+            for j in range(PACK):
+                for g in range(D_PASSES):
+                    mx(
+                        bank[:, j * P : (j + 1) * P],
+                        td_q,
+                        slice((j * D_PASSES + g) * P, (j * D_PASSES + g + 1) * P),
+                        quantised[("pred", i)],
+                        slice(g * P, (g + 1) * P),
+                        start=(g == 0),
+                        stop=(g == D_PASSES - 1),
+                    )
+            vip = grouped_pool.tile([P, BANK], BF16, tag="vip", align_bytes=64)
+            nc.scalar.activation(
+                out=vip[:].rearrange("p (b j) -> p b j", j=PACK),
+                in_=bank[:].rearrange("p (j b) -> p b j", j=PACK),
+                func=RELU,
+            )
+            grouped_of[("vip", i)] = vip
+
+        def som_matmuls(i):
+            feed = psum.tile([P, BANK], F32, tag="bank")
+            for g in range(D_PASSES):
+                mx(
+                    feed[:],
+                    quantised[("x", i)],
+                    slice(g * P, (g + 1) * P),
+                    som_q,
+                    slice(g * CELLS, (g + 1) * CELLS),
+                    start=(g == 0),
+                    stop=(g == D_PASSES - 1),
+                )
+            som_ff = som_pool.tile([P, CELLS], F32)
+            nc.scalar.activation(out=som_ff[:], in_=feed[:], func=RELU)
+            inhibition = psum.tile([P, BANK], F32, tag="bank")
+            mx(
+                inhibition[:],
+                quantised[("vip", i)],
+                slice(0, P),
+                vs_q,
+                slice(0, CELLS),
+                start=True,
+                stop=True,
+            )
+            result = out_pool.tile([P, CELLS], F32)
+            nc.vector.tensor_tensor(out=result[:], in0=som_ff[:], in1=inhibition[:], op=SUBTRACT)
+            nc.gpsimd.tensor_scalar(
+                out=result[:], in0=result[:], scalar1=float("inf"), scalar2=0.0, op0=MIN, op1=MAX
+            )
+            c, t = divmod(i, CHUNK_TILES)
+            nc.sync.dma_start(out=out_chunks[c][:, t * CELLS : (t + 1) * CELLS], in_=result[:])
+
+        load_td()
+        for r in range(LOAD_AHEAD):
+            loads_for_round(r)
+        prepare_td()
+
+        for r in range(UNITS + X_LAG + 2):
+            loads_for_round(r + LOAD_AHEAD)
+            if r == X_LAG + 1:
+                prepare_som_and_vs()
+
+            for i in tiles_of(r):
+                flip_tile("pred", i, nc.scalar.copy)
+            for i in tiles_of(r - 1 - X_LAG):
+                by_vector = i % VECTOR_SHARE == VECTOR_SHARE - 1
+                flip_tile("x", i, nc.vector.tensor_copy if by_vector else nc.scalar.copy)
+            for i in tiles_of(r):
+                quantise_tile("pred", i, codes_pool)
+            for i in tiles_of(r - 1 - X_LAG):
+                quantise_tile("x", i, codes_pool)
+
+            for i in tiles_of(r - 1):
+                vip_matmul(i)
+            for i in tiles_of(r - 1):
+                quantise_tile("vip", i, vip_pool)
+            for i in tiles_of(r - 2 - X_LAG):
+                som_matmuls(i)

@@ -50,6 +50,7 @@ def tile_pecircuits_pa_t_kernel(
         raw_pool = stack.enter_context(
             tc.tile_pool(name="raw", bufs=(LOAD_AHEAD + 1) * ROUND_CHUNKS)
         )
+        sorted_pool = stack.enter_context(tc.tile_pool(name="sorted", bufs=2 * ROUND_CHUNKS))
         grouped_pool = stack.enter_context(tc.tile_pool(name="grouped", bufs=3 * ROUND_TILES))
         codes_pool = stack.enter_context(tc.tile_pool(name="codes", bufs=3 * ROUND_TILES))
         vip_pool = stack.enter_context(
@@ -66,15 +67,15 @@ def tile_pecircuits_pa_t_kernel(
         def as_pairs(words):
             return words.rearrange("p (g b u) -> p g b u", g=D_PASSES, u=2)
 
-        def flip(words, dest, copy_out):
+        def every_second(words):
+            return [
+                words[:, 2 * g * P + u : 2 * (g + 1) * P : 2] for g in range(D_PASSES) for u in range(2)
+            ]
+
+        def flip(blocks, dest, copy_out):
             bank = psum.tile([P, BANK], F32, tag="bank")
             for c in range(BLOCKS):
-                g, u = divmod(c, 2)
-                nc.tensor.transpose(
-                    bank[:, c * P : (c + 1) * P],
-                    words[:, 2 * g * P + u : 2 * (g + 1) * P : 2],
-                    ident[:],
-                )
+                nc.tensor.transpose(bank[:, c * P : (c + 1) * P], blocks[c], ident[:])
             copy_out(out=dest, in_=bank[:].rearrange("p (g u b) -> p g b u", g=D_PASSES, u=2))
 
         def quantise(grouped, codes, scales):
@@ -123,7 +124,7 @@ def tile_pecircuits_pa_t_kernel(
             for j in range(PACK):
                 grouped = grouped_pool.tile([P, 2 * BANK], BF16, tag="grouped", align_bytes=64)
                 flip(
-                    td_raw[:].bitcast(F32)[:, j * BANK : (j + 1) * BANK],
+                    every_second(td_raw[:].bitcast(F32)[:, j * BANK : (j + 1) * BANK]),
                     as_pairs(grouped[:].bitcast(F32)),
                     either_copy(j),
                 )
@@ -148,14 +149,14 @@ def tile_pecircuits_pa_t_kernel(
             )
             for r in range(BLOCKS):
                 flip(
-                    som_raw[:].bitcast(F32)[:, r * BANK : (r + 1) * BANK],
+                    every_second(som_raw[:].bitcast(F32)[:, r * BANK : (r + 1) * BANK]),
                     som_words[:, r],
                     either_copy(r),
                 )
             for h in range(2):
                 half = slice(h * BANK, (h + 1) * BANK)
                 flip(
-                    vs_raw[:].bitcast(F32)[:, half],
+                    every_second(vs_raw[:].bitcast(F32)[:, half]),
                     as_pairs(vs_grouped[:].bitcast(F32)[:, half]),
                     either_copy(h),
                 )
@@ -163,6 +164,7 @@ def tile_pecircuits_pa_t_kernel(
             quantise(vs_grouped[:], vs_q[0][:], vs_q[1][:])
 
         raw = {}
+        sorted_words = {}
         grouped_of = {}
         quantised = {}
 
@@ -187,11 +189,22 @@ def tile_pecircuits_pa_t_kernel(
             for c in chunks_of(r - 1 - X_LAG):
                 load("x", x_chunks, c)
 
+        def sort_chunk(name, c):
+            words = sorted_pool.tile([P, CHUNK_TILES * BANK], F32, tag=name + "_sorted")
+            nc.vector.tensor_copy(
+                out=words[:].rearrange("p (u w) -> p u w", u=2),
+                in_=raw[(name, c)][:].bitcast(F32).rearrange("p (w u) -> p u w", u=2),
+            )
+            sorted_words[(name, c)] = words
+
         def flip_tile(name, i, copy_out):
             c, t = divmod(i, CHUNK_TILES)
             grouped = grouped_pool.tile([P, 2 * BANK], BF16, tag="grouped", align_bytes=64)
+            words = sorted_words[(name, c)][:].rearrange(
+                "p (u b w) -> p b u w", u=2, b=CHUNK_TILES * D_PASSES
+            )
             flip(
-                raw[(name, c)][:].bitcast(F32)[:, t * BANK : (t + 1) * BANK],
+                [words[:, t * D_PASSES + g, u, :] for g in range(D_PASSES) for u in range(2)],
                 as_pairs(grouped[:].bitcast(F32)),
                 copy_out,
             )
@@ -261,6 +274,8 @@ def tile_pecircuits_pa_t_kernel(
         load_td()
         for r in range(LOAD_AHEAD):
             loads_for_round(r)
+        for c in chunks_of(0):
+            sort_chunk("pred", c)
         prepare_td()
 
         for r in range(UNITS + X_LAG + 2):
@@ -270,11 +285,15 @@ def tile_pecircuits_pa_t_kernel(
 
             for i in tiles_of(r):
                 flip_tile("pred", i, nc.scalar.copy)
+            for c in chunks_of(r + 1):
+                sort_chunk("pred", c)
             for i in tiles_of(r - 1 - X_LAG):
                 by_vector = i % VECTOR_SHARE == VECTOR_SHARE - 1
                 flip_tile("x", i, nc.vector.tensor_copy if by_vector else nc.scalar.copy)
             for i in tiles_of(r):
                 quantise_tile("pred", i, codes_pool)
+            for c in chunks_of(r - X_LAG):
+                sort_chunk("x", c)
             for i in tiles_of(r - 1 - X_LAG):
                 quantise_tile("x", i, codes_pool)
 

@@ -28,12 +28,7 @@ BLOCKS = BANK // P
 TILES = BATCH // P
 CHUNK_TILES = 2
 CHUNKS = TILES // CHUNK_TILES
-ROUND_CHUNKS = 2
-ROUND_TILES = ROUND_CHUNKS * CHUNK_TILES
-UNITS = CHUNKS // ROUND_CHUNKS
-X_LAG = 1
-LOAD_AHEAD = 2
-VECTOR_SHARE = 2
+LOAD_AHEAD = 3
 
 
 def tile_pecircuits_pa_t_kernel(
@@ -47,15 +42,10 @@ def tile_pecircuits_pa_t_kernel(
 
     with ExitStack() as stack:
         const = stack.enter_context(tc.tile_pool(name="const", bufs=1))
-        raw_pool = stack.enter_context(
-            tc.tile_pool(name="raw", bufs=(LOAD_AHEAD + 1) * ROUND_CHUNKS)
-        )
-        sorted_pool = stack.enter_context(tc.tile_pool(name="sorted", bufs=2 * ROUND_CHUNKS))
-        grouped_pool = stack.enter_context(tc.tile_pool(name="grouped", bufs=3 * ROUND_TILES))
-        codes_pool = stack.enter_context(tc.tile_pool(name="codes", bufs=3 * ROUND_TILES))
-        vip_pool = stack.enter_context(
-            tc.tile_pool(name="vip", bufs=(X_LAG + 3) * ROUND_TILES)
-        )
+        raw_pool = stack.enter_context(tc.tile_pool(name="raw", bufs=LOAD_AHEAD + 2))
+        sorted_pool = stack.enter_context(tc.tile_pool(name="sorted", bufs=3))
+        grouped_pool = stack.enter_context(tc.tile_pool(name="grouped", bufs=4))
+        codes_pool = stack.enter_context(tc.tile_pool(name="codes", bufs=4))
         som_pool = stack.enter_context(tc.tile_pool(name="som", bufs=4))
         out_pool = stack.enter_context(tc.tile_pool(name="result", bufs=6))
         psum = stack.enter_context(tc.psum_pool(name="psum", bufs=8))
@@ -167,85 +157,83 @@ def tile_pecircuits_pa_t_kernel(
         sorted_words = {}
         grouped_of = {}
         quantised = {}
+        source = {"pred": pred_chunks, "x": x_chunks}
 
-        def chunks_of(unit):
-            if 0 <= unit < UNITS:
-                return range(unit * ROUND_CHUNKS, (unit + 1) * ROUND_CHUNKS)
-            return range(0)
+        def exists(c):
+            return 0 <= c < CHUNKS
 
-        def tiles_of(unit):
-            return [c * CHUNK_TILES + t for c in chunks_of(unit) for t in range(CHUNK_TILES)]
-
-        def load(name, chunks, c):
-            rows = raw_pool.tile([P, CHUNK_TILES * D_IN], BF16, tag=name + "_raw")
-            nc.sync.dma_start(out=rows[:], in_=chunks[c])
-            raw[(name, c)] = rows
-
-        def loads_for_round(r):
-            if r == X_LAG + 1:
-                load_som_and_vs()
-            for c in chunks_of(r):
-                load("pred", pred_chunks, c)
-            for c in chunks_of(r - 1 - X_LAG):
-                load("x", x_chunks, c)
+        def load(name, c):
+            if exists(c):
+                rows = raw_pool.tile([P, CHUNK_TILES * D_IN], BF16, tag=name + "_raw")
+                nc.sync.dma_start(out=rows[:], in_=source[name][c])
+                raw[(name, c)] = rows
 
         def sort_chunk(name, c):
-            words = sorted_pool.tile([P, CHUNK_TILES * BANK], F32, tag=name + "_sorted")
-            nc.vector.tensor_copy(
-                out=words[:].rearrange("p (u w) -> p u w", u=2),
-                in_=raw[(name, c)][:].bitcast(F32).rearrange("p (w u) -> p u w", u=2),
-            )
-            sorted_words[(name, c)] = words
+            if exists(c):
+                words = sorted_pool.tile([P, CHUNK_TILES * BANK], F32, tag=name + "_sorted")
+                nc.vector.tensor_copy(
+                    out=words[:].rearrange("p (u w) -> p u w", u=2),
+                    in_=raw[(name, c)][:].bitcast(F32).rearrange("p (w u) -> p u w", u=2),
+                )
+                sorted_words[(name, c)] = words
 
-        def flip_tile(name, i, copy_out):
-            c, t = divmod(i, CHUNK_TILES)
-            grouped = grouped_pool.tile([P, 2 * BANK], BF16, tag="grouped", align_bytes=64)
-            words = sorted_words[(name, c)][:].rearrange(
-                "p (u b w) -> p b u w", u=2, b=CHUNK_TILES * D_PASSES
-            )
-            flip(
-                [words[:, t * D_PASSES + g, u, :] for g in range(D_PASSES) for u in range(2)],
-                as_pairs(grouped[:].bitcast(F32)),
-                copy_out,
-            )
-            grouped_of[(name, i)] = grouped
-
-        def quantise_tile(name, i, pool):
-            grouped = grouped_of[(name, i)]
-            width = grouped.shape[1] // PACK
-            codes = pool.tile([P, width], U32, tag=name + "_codes", align_bytes=64)
-            scales = pool.tile([P, width], U8, tag=name + "_scales", align_bytes=64)
-            quantise(grouped[:], codes[:], scales[:])
-            quantised[(name, i)] = (codes, scales)
-
-        def vip_matmul(i):
-            bank = psum.tile([P, BANK], F32, tag="bank")
-            for j in range(PACK):
-                for g in range(D_PASSES):
-                    mx(
-                        bank[:, j * P : (j + 1) * P],
-                        td_q,
-                        slice((j * D_PASSES + g) * P, (j * D_PASSES + g + 1) * P),
-                        quantised[("pred", i)],
-                        slice(g * P, (g + 1) * P),
-                        start=(g == 0),
-                        stop=(g == D_PASSES - 1),
+        def flip_chunk(name, c, copies):
+            if exists(c):
+                grouped = grouped_pool.tile(
+                    [P, CHUNK_TILES * D_IN], BF16, tag="grouped_chunk", align_bytes=64
+                )
+                words = sorted_words[(name, c)][:].rearrange(
+                    "p (u b w) -> p b u w", u=2, b=CHUNK_TILES * D_PASSES
+                )
+                for t in range(CHUNK_TILES):
+                    flip(
+                        [words[:, t * D_PASSES + g, u, :] for g in range(D_PASSES) for u in range(2)],
+                        as_pairs(grouped[:].bitcast(F32)[:, t * BANK : (t + 1) * BANK]),
+                        copies[t],
                     )
-            vip = grouped_pool.tile([P, BANK], BF16, tag="vip", align_bytes=64)
-            nc.scalar.activation(
-                out=vip[:].rearrange("p (b j) -> p b j", j=PACK),
-                in_=bank[:].rearrange("p (j b) -> p b j", j=PACK),
-                func=RELU,
-            )
-            grouped_of[("vip", i)] = vip
+                grouped_of[(name, c)] = grouped
 
-        def som_matmuls(i):
+        def quantise_chunk(name, c):
+            if exists(c):
+                grouped = grouped_of[(name, c)]
+                width = grouped.shape[1] // PACK
+                codes = codes_pool.tile([P, width], U32, tag=name + "_codes", align_bytes=64)
+                scales = codes_pool.tile([P, width], U8, tag=name + "_scales", align_bytes=64)
+                quantise(grouped[:], codes[:], scales[:])
+                quantised[(name, c)] = (codes, scales)
+
+        def vip_matmuls(c):
+            if exists(c):
+                vip = grouped_pool.tile([P, CHUNK_TILES * BANK], BF16, tag="vip", align_bytes=64)
+                for t in range(CHUNK_TILES):
+                    bank = psum.tile([P, BANK], F32, tag="bank")
+                    for j in range(PACK):
+                        for g in range(D_PASSES):
+                            mx(
+                                bank[:, j * P : (j + 1) * P],
+                                td_q,
+                                slice((j * D_PASSES + g) * P, (j * D_PASSES + g + 1) * P),
+                                quantised[("pred", c)],
+                                slice((t * D_PASSES + g) * P, (t * D_PASSES + g + 1) * P),
+                                start=(g == 0),
+                                stop=(g == D_PASSES - 1),
+                            )
+                    nc.scalar.activation(
+                        out=vip[:, t * BANK : (t + 1) * BANK].rearrange("p (b j) -> p b j", j=PACK),
+                        in_=bank[:].rearrange("p (j b) -> p b j", j=PACK),
+                        func=RELU,
+                    )
+                grouped_of[("vip", c)] = vip
+
+        def som_matmuls(c, t):
+            if not exists(c):
+                return
             feed = psum.tile([P, BANK], F32, tag="bank")
             for g in range(D_PASSES):
                 mx(
                     feed[:],
-                    quantised[("x", i)],
-                    slice(g * P, (g + 1) * P),
+                    quantised[("x", c)],
+                    slice((t * D_PASSES + g) * P, (t * D_PASSES + g + 1) * P),
                     som_q,
                     slice(g * CELLS, (g + 1) * CELLS),
                     start=(g == 0),
@@ -256,8 +244,8 @@ def tile_pecircuits_pa_t_kernel(
             inhibition = psum.tile([P, BANK], F32, tag="bank")
             mx(
                 inhibition[:],
-                quantised[("vip", i)],
-                slice(0, P),
+                quantised[("vip", c)],
+                slice(t * P, (t + 1) * P),
                 vs_q,
                 slice(0, CELLS),
                 start=True,
@@ -268,38 +256,32 @@ def tile_pecircuits_pa_t_kernel(
             nc.gpsimd.tensor_scalar(
                 out=result[:], in0=result[:], scalar1=float("inf"), scalar2=0.0, op0=MIN, op1=MAX
             )
-            c, t = divmod(i, CHUNK_TILES)
             nc.sync.dma_start(out=out_chunks[c][:, t * CELLS : (t + 1) * CELLS], in_=result[:])
 
         load_td()
-        for r in range(LOAD_AHEAD):
-            loads_for_round(r)
-        for c in chunks_of(0):
-            sort_chunk("pred", c)
+        load("pred", 0)
+        load("pred", 1)
+        load("x", 0)
+        load("pred", 2)
+        load("x", 1)
+        load_som_and_vs()
+        sort_chunk("pred", 0)
         prepare_td()
 
-        for r in range(UNITS + X_LAG + 2):
-            loads_for_round(r + LOAD_AHEAD)
-            if r == X_LAG + 1:
+        for r in range(CHUNKS + 2):
+            load("pred", r + LOAD_AHEAD)
+            load("x", r + LOAD_AHEAD - 1)
+
+            sort_chunk("pred", r + 1)
+            sort_chunk("x", r)
+            flip_chunk("pred", r, [nc.scalar.copy, nc.scalar.copy])
+            flip_chunk("x", r - 1, [nc.scalar.copy, nc.vector.tensor_copy])
+            quantise_chunk("pred", r)
+            quantise_chunk("x", r - 1)
+            if r == 2:
                 prepare_som_and_vs()
 
-            for i in tiles_of(r):
-                flip_tile("pred", i, nc.scalar.copy)
-            for c in chunks_of(r + 1):
-                sort_chunk("pred", c)
-            for i in tiles_of(r - 1 - X_LAG):
-                by_vector = i % VECTOR_SHARE == VECTOR_SHARE - 1
-                flip_tile("x", i, nc.vector.tensor_copy if by_vector else nc.scalar.copy)
-            for i in tiles_of(r):
-                quantise_tile("pred", i, codes_pool)
-            for c in chunks_of(r - X_LAG):
-                sort_chunk("x", c)
-            for i in tiles_of(r - 1 - X_LAG):
-                quantise_tile("x", i, codes_pool)
-
-            for i in tiles_of(r - 1):
-                vip_matmul(i)
-            for i in tiles_of(r - 1):
-                quantise_tile("vip", i, vip_pool)
-            for i in tiles_of(r - 2 - X_LAG):
-                som_matmuls(i)
+            vip_matmuls(r - 1)
+            quantise_chunk("vip", r - 1)
+            for t in range(CHUNK_TILES):
+                som_matmuls(r - 2, t)

@@ -28,7 +28,12 @@ BLOCKS = BANK // P
 TILES = BATCH // P
 CHUNK_TILES = 2
 CHUNKS = TILES // CHUNK_TILES
+HEAD_CHUNKS = 4
+ROUND_CHUNKS = 2
+X_LAG = 3
 LOAD_AHEAD = 3
+UNSORTED = 2
+VECTOR_SHARE = 4
 
 
 def tile_pecircuits_pa_t_kernel(
@@ -42,10 +47,17 @@ def tile_pecircuits_pa_t_kernel(
 
     with ExitStack() as stack:
         const = stack.enter_context(tc.tile_pool(name="const", bufs=1))
-        raw_pool = stack.enter_context(tc.tile_pool(name="raw", bufs=LOAD_AHEAD + 2))
-        sorted_pool = stack.enter_context(tc.tile_pool(name="sorted", bufs=3))
-        grouped_pool = stack.enter_context(tc.tile_pool(name="grouped", bufs=4))
-        codes_pool = stack.enter_context(tc.tile_pool(name="codes", bufs=4))
+        raw_pool = stack.enter_context(
+            tc.tile_pool(name="raw", bufs=(LOAD_AHEAD + 1) * ROUND_CHUNKS - 1)
+        )
+        sorted_pool = stack.enter_context(tc.tile_pool(name="sorted", bufs=2 * ROUND_CHUNKS))
+        grouped_pool = stack.enter_context(
+            tc.tile_pool(name="grouped", bufs=3 * ROUND_CHUNKS)
+        )
+        codes_pool = stack.enter_context(tc.tile_pool(name="codes", bufs=3 * ROUND_CHUNKS))
+        vip_pool = stack.enter_context(
+            tc.tile_pool(name="vip", bufs=(X_LAG + 2) * ROUND_CHUNKS)
+        )
         som_pool = stack.enter_context(tc.tile_pool(name="som", bufs=4))
         out_pool = stack.enter_context(tc.tile_pool(name="result", bufs=6))
         psum = stack.enter_context(tc.psum_pool(name="psum", bufs=8))
@@ -105,23 +117,27 @@ def tile_pecircuits_pa_t_kernel(
 
         def load_td():
             rows = W_vip_td.rearrange("(q j) k -> q (j k)", j=PACK)
-            for u in range(2):
-                half = slice(u * 2 * D_IN, (u + 1) * 2 * D_IN)
-                nc.sync.dma_start(out=td_raw[:, half], in_=rows[:, half])
+            for j in range(PACK):
+                row = slice(j * D_IN, (j + 1) * D_IN)
+                nc.sync.dma_start(out=td_raw[:, row], in_=rows[:, row])
 
         def prepare_td():
-            tiles = []
-            for j in range(PACK):
-                grouped = grouped_pool.tile([P, 2 * BANK], BF16, tag="grouped", align_bytes=64)
-                flip(
-                    every_second(td_raw[:].bitcast(F32)[:, j * BANK : (j + 1) * BANK]),
-                    as_pairs(grouped[:].bitcast(F32)),
-                    either_copy(j),
+            pairs = []
+            for h in range(2):
+                grouped = grouped_pool.tile(
+                    [P, CHUNK_TILES * D_IN], BF16, tag="grouped_chunk", align_bytes=64
                 )
-                tiles.append(grouped)
-            for j in range(PACK):
-                cols = slice(j * D_PASSES * P, (j + 1) * D_PASSES * P)
-                quantise(tiles[j][:], td_q[0][:, cols], td_q[1][:, cols])
+                for t in range(2):
+                    j = 2 * h + t
+                    flip(
+                        every_second(td_raw[:].bitcast(F32)[:, j * BANK : (j + 1) * BANK]),
+                        as_pairs(grouped[:].bitcast(F32)[:, t * BANK : (t + 1) * BANK]),
+                        either_copy(t),
+                    )
+                pairs.append(grouped)
+            for h in range(2):
+                cols = slice(h * 2 * D_PASSES * P, (h + 1) * 2 * D_PASSES * P)
+                quantise(pairs[h][:], td_q[0][:, cols], td_q[1][:, cols])
 
         def load_som_and_vs():
             nc.sync.dma_start(
@@ -159,75 +175,70 @@ def tile_pecircuits_pa_t_kernel(
         quantised = {}
         source = {"pred": pred_chunks, "x": x_chunks}
 
-        def exists(c):
-            return 0 <= c < CHUNKS
-
         def load(name, c):
-            if exists(c):
-                rows = raw_pool.tile([P, CHUNK_TILES * D_IN], BF16, tag=name + "_raw")
-                nc.sync.dma_start(out=rows[:], in_=source[name][c])
-                raw[(name, c)] = rows
+            rows = raw_pool.tile([P, CHUNK_TILES * D_IN], BF16, tag=name + "_raw")
+            nc.sync.dma_start(out=rows[:], in_=source[name][c])
+            raw[(name, c)] = rows
 
         def sort_chunk(name, c):
-            if exists(c):
-                words = sorted_pool.tile([P, CHUNK_TILES * BANK], F32, tag=name + "_sorted")
-                nc.vector.tensor_copy(
-                    out=words[:].rearrange("p (u w) -> p u w", u=2),
-                    in_=raw[(name, c)][:].bitcast(F32).rearrange("p (w u) -> p u w", u=2),
-                )
-                sorted_words[(name, c)] = words
+            words = sorted_pool.tile([P, CHUNK_TILES * BANK], F32, tag=name + "_sorted")
+            nc.vector.tensor_copy(
+                out=words[:].rearrange("p (u w) -> p u w", u=2),
+                in_=raw[(name, c)][:].bitcast(F32).rearrange("p (w u) -> p u w", u=2),
+            )
+            sorted_words[(name, c)] = words
 
         def flip_chunk(name, c, copies):
-            if exists(c):
-                grouped = grouped_pool.tile(
-                    [P, CHUNK_TILES * D_IN], BF16, tag="grouped_chunk", align_bytes=64
+            grouped = grouped_pool.tile(
+                [P, CHUNK_TILES * D_IN], BF16, tag="grouped_chunk", align_bytes=64
+            )
+            if (name, c) in sorted_words:
+                halves = sorted_words[(name, c)][:].rearrange("p (u w) -> p u w", u=2)
+            else:
+                halves = raw[(name, c)][:].bitcast(F32).rearrange("p (w u) -> p u w", u=2)
+            for t in range(CHUNK_TILES):
+                starts = [(t * D_PASSES + g) * P for g in range(D_PASSES)]
+                flip(
+                    [halves[:, u, w : w + P] for w in starts for u in range(2)],
+                    as_pairs(grouped[:].bitcast(F32)[:, t * BANK : (t + 1) * BANK]),
+                    copies[t],
                 )
-                words = sorted_words[(name, c)][:].rearrange(
-                    "p (u b w) -> p b u w", u=2, b=CHUNK_TILES * D_PASSES
-                )
-                for t in range(CHUNK_TILES):
-                    flip(
-                        [words[:, t * D_PASSES + g, u, :] for g in range(D_PASSES) for u in range(2)],
-                        as_pairs(grouped[:].bitcast(F32)[:, t * BANK : (t + 1) * BANK]),
-                        copies[t],
-                    )
-                grouped_of[(name, c)] = grouped
+            grouped_of[(name, c)] = grouped
 
         def quantise_chunk(name, c):
-            if exists(c):
-                grouped = grouped_of[(name, c)]
-                width = grouped.shape[1] // PACK
-                codes = codes_pool.tile([P, width], U32, tag=name + "_codes", align_bytes=64)
-                scales = codes_pool.tile([P, width], U8, tag=name + "_scales", align_bytes=64)
-                quantise(grouped[:], codes[:], scales[:])
-                quantised[(name, c)] = (codes, scales)
+            grouped = grouped_of[(name, c)]
+            width = grouped.shape[1] // PACK
+            pool = vip_pool if name == "vip" else codes_pool
+            codes = pool.tile([P, width], U32, tag=name + "_codes", align_bytes=64)
+            scales = pool.tile([P, width], U8, tag=name + "_scales", align_bytes=64)
+            quantise(grouped[:], codes[:], scales[:])
+            quantised[(name, c)] = (codes, scales)
 
         def vip_matmuls(c):
-            if exists(c):
-                vip = grouped_pool.tile([P, CHUNK_TILES * BANK], BF16, tag="vip", align_bytes=64)
-                for t in range(CHUNK_TILES):
-                    bank = psum.tile([P, BANK], F32, tag="bank")
-                    for j in range(PACK):
-                        for g in range(D_PASSES):
-                            mx(
-                                bank[:, j * P : (j + 1) * P],
-                                td_q,
-                                slice((j * D_PASSES + g) * P, (j * D_PASSES + g + 1) * P),
-                                quantised[("pred", c)],
-                                slice((t * D_PASSES + g) * P, (t * D_PASSES + g + 1) * P),
-                                start=(g == 0),
-                                stop=(g == D_PASSES - 1),
-                            )
-                    nc.scalar.activation(
-                        out=vip[:, t * BANK : (t + 1) * BANK].rearrange("p (b j) -> p b j", j=PACK),
-                        in_=bank[:].rearrange("p (j b) -> p b j", j=PACK),
-                        func=RELU,
-                    )
-                grouped_of[("vip", c)] = vip
+            vip = grouped_pool.tile([P, CHUNK_TILES * BANK], BF16, tag="vip", align_bytes=64)
+            for t in range(CHUNK_TILES):
+                bank = psum.tile([P, BANK], F32, tag="bank")
+                for j in range(PACK):
+                    for g in range(D_PASSES):
+                        mx(
+                            bank[:, j * P : (j + 1) * P],
+                            td_q,
+                            slice((j * D_PASSES + g) * P, (j * D_PASSES + g + 1) * P),
+                            quantised[("pred", c)],
+                            slice((t * D_PASSES + g) * P, (t * D_PASSES + g + 1) * P),
+                            start=(g == 0),
+                            stop=(g == D_PASSES - 1),
+                        )
+                nc.scalar.activation(
+                    out=vip[:, t * BANK : (t + 1) * BANK].rearrange("p (b j) -> p b j", j=PACK),
+                    in_=bank[:].rearrange("p (j b) -> p b j", j=PACK),
+                    func=RELU,
+                )
+            grouped_of[("vip", c)] = vip
 
-        def som_matmuls(c, t):
-            if not exists(c):
-                return
+        som_ff = {}
+
+        def feed_matmul(c, t):
             feed = psum.tile([P, BANK], F32, tag="bank")
             for g in range(D_PASSES):
                 mx(
@@ -239,8 +250,11 @@ def tile_pecircuits_pa_t_kernel(
                     start=(g == 0),
                     stop=(g == D_PASSES - 1),
                 )
-            som_ff = som_pool.tile([P, CELLS], F32)
-            nc.scalar.activation(out=som_ff[:], in_=feed[:], func=RELU)
+            fed = som_pool.tile([P, CELLS], F32)
+            nc.scalar.activation(out=fed[:], in_=feed[:], func=RELU)
+            som_ff[(c, t)] = fed
+
+        def inhibit(c, t):
             inhibition = psum.tile([P, BANK], F32, tag="bank")
             mx(
                 inhibition[:],
@@ -252,36 +266,81 @@ def tile_pecircuits_pa_t_kernel(
                 stop=True,
             )
             result = out_pool.tile([P, CELLS], F32)
-            nc.vector.tensor_tensor(out=result[:], in0=som_ff[:], in1=inhibition[:], op=SUBTRACT)
-            nc.gpsimd.tensor_scalar(
-                out=result[:], in0=result[:], scalar1=float("inf"), scalar2=0.0, op0=MIN, op1=MAX
-            )
-            nc.sync.dma_start(out=out_chunks[c][:, t * CELLS : (t + 1) * CELLS], in_=result[:])
+            ends_kernel = (c, t) == (CHUNKS - 1, CHUNK_TILES - 1)
+            parts = 2 if ends_kernel else 1
+            relu_engine = nc.vector if ends_kernel else nc.gpsimd
+            for h in range(parts):
+                cols = slice(h * CELLS // parts, (h + 1) * CELLS // parts)
+                nc.vector.tensor_tensor(
+                    out=result[:, cols],
+                    in0=som_ff[(c, t)][:, cols],
+                    in1=inhibition[:, cols],
+                    op=SUBTRACT,
+                )
+                relu_engine.tensor_scalar(
+                    out=result[:, cols],
+                    in0=result[:, cols],
+                    scalar1=float("inf"),
+                    scalar2=0.0,
+                    op0=MIN,
+                    op1=MAX,
+                )
+                rows = out_chunks[c][:, t * CELLS : (t + 1) * CELLS]
+                nc.sync.dma_start(out=rows[:, cols], in_=result[:, cols])
 
+        units = [[c] for c in range(HEAD_CHUNKS)]
+        units += [
+            list(range(c, c + ROUND_CHUNKS)) for c in range(HEAD_CHUNKS, CHUNKS, ROUND_CHUNKS)
+        ]
+
+        def unit(u):
+            return units[u] if 0 <= u < len(units) else []
+
+        def loads_for_round(r):
+            for c in unit(r):
+                load("pred", c)
+            if r == X_LAG:
+                load_som_and_vs()
+            for c in unit(r - X_LAG):
+                load("x", c)
+
+        loads_for_round(0)
         load_td()
-        load("pred", 0)
-        load("pred", 1)
-        load("x", 0)
-        load("pred", 2)
-        load("x", 1)
-        load_som_and_vs()
-        sort_chunk("pred", 0)
+        for r in range(1, LOAD_AHEAD):
+            loads_for_round(r)
+        flip_chunk("pred", 0, [nc.scalar.copy] * CHUNK_TILES)
+        quantise_chunk("pred", 0)
         prepare_td()
 
-        for r in range(CHUNKS + 2):
-            load("pred", r + LOAD_AHEAD)
-            load("x", r + LOAD_AHEAD - 1)
+        for r in range(len(units) + X_LAG + 1):
+            loads_for_round(r + LOAD_AHEAD)
 
-            sort_chunk("pred", r + 1)
-            sort_chunk("x", r)
-            flip_chunk("pred", r, [nc.scalar.copy, nc.scalar.copy])
-            flip_chunk("x", r - 1, [nc.scalar.copy, nc.vector.tensor_copy])
-            quantise_chunk("pred", r)
-            quantise_chunk("x", r - 1)
-            if r == 2:
+            fresh = unit(r) if r > 0 else []
+            for c in fresh:
+                by_vector = c % VECTOR_SHARE == VECTOR_SHARE - 1
+                flip_chunk(
+                    "pred", c, [nc.scalar.copy, nc.vector.tensor_copy if by_vector else nc.scalar.copy]
+                )
+            for c in unit(r + 1):
+                if c >= UNSORTED:
+                    sort_chunk("pred", c)
+            for c in unit(r - X_LAG):
+                flip_chunk("x", c, [nc.scalar.copy] * CHUNK_TILES)
+            for c in fresh:
+                quantise_chunk("pred", c)
+            for c in unit(r - X_LAG + 1):
+                sort_chunk("x", c)
+            for c in unit(r - X_LAG):
+                quantise_chunk("x", c)
+            if r == X_LAG:
                 prepare_som_and_vs()
 
-            vip_matmuls(r - 1)
-            quantise_chunk("vip", r - 1)
-            for t in range(CHUNK_TILES):
-                som_matmuls(r - 2, t)
+            for c in unit(r - 1):
+                vip_matmuls(c)
+            for c in unit(r - 1):
+                quantise_chunk("vip", c)
+            for c in unit(r - X_LAG - 1):
+                for t in range(CHUNK_TILES):
+                    feed_matmul(c, t)
+                for t in range(CHUNK_TILES):
+                    inhibit(c, t)

@@ -28,12 +28,11 @@ BLOCKS = BANK // P
 TILES = BATCH // P
 CHUNK_TILES = 2
 CHUNKS = TILES // CHUNK_TILES
-HEAD_CHUNKS = 4
+HEAD_CHUNKS = 6
 ROUND_CHUNKS = 2
 X_LAG = 3
 LOAD_AHEAD = 3
 UNSORTED = 2
-VECTOR_SHARE = 4
 
 
 def tile_pecircuits_pa_t_kernel(
@@ -266,27 +265,13 @@ def tile_pecircuits_pa_t_kernel(
                 stop=True,
             )
             result = out_pool.tile([P, CELLS], F32)
-            ends_kernel = (c, t) == (CHUNKS - 1, CHUNK_TILES - 1)
-            parts = 2 if ends_kernel else 1
-            relu_engine = nc.vector if ends_kernel else nc.gpsimd
-            for h in range(parts):
-                cols = slice(h * CELLS // parts, (h + 1) * CELLS // parts)
-                nc.vector.tensor_tensor(
-                    out=result[:, cols],
-                    in0=som_ff[(c, t)][:, cols],
-                    in1=inhibition[:, cols],
-                    op=SUBTRACT,
-                )
-                relu_engine.tensor_scalar(
-                    out=result[:, cols],
-                    in0=result[:, cols],
-                    scalar1=float("inf"),
-                    scalar2=0.0,
-                    op0=MIN,
-                    op1=MAX,
-                )
-                rows = out_chunks[c][:, t * CELLS : (t + 1) * CELLS]
-                nc.sync.dma_start(out=rows[:, cols], in_=result[:, cols])
+            nc.vector.tensor_tensor(
+                out=result[:], in0=som_ff[(c, t)][:], in1=inhibition[:], op=SUBTRACT
+            )
+            nc.gpsimd.tensor_scalar(
+                out=result[:], in0=result[:], scalar1=float("inf"), scalar2=0.0, op0=MIN, op1=MAX
+            )
+            nc.sync.dma_start(out=out_chunks[c][:, t * CELLS : (t + 1) * CELLS], in_=result[:])
 
         units = [[c] for c in range(HEAD_CHUNKS)]
         units += [
@@ -299,10 +284,10 @@ def tile_pecircuits_pa_t_kernel(
         def loads_for_round(r):
             for c in unit(r):
                 load("pred", c)
-            if r == X_LAG:
-                load_som_and_vs()
             for c in unit(r - X_LAG):
                 load("x", c)
+            if r == X_LAG:
+                load_som_and_vs()
 
         loads_for_round(0)
         load_td()
@@ -317,10 +302,8 @@ def tile_pecircuits_pa_t_kernel(
 
             fresh = unit(r) if r > 0 else []
             for c in fresh:
-                by_vector = c % VECTOR_SHARE == VECTOR_SHARE - 1
-                flip_chunk(
-                    "pred", c, [nc.scalar.copy, nc.vector.tensor_copy if by_vector else nc.scalar.copy]
-                )
+                first = nc.vector.tensor_copy if c == fresh[0] else nc.scalar.copy
+                flip_chunk("pred", c, [first, nc.scalar.copy])
             for c in unit(r + 1):
                 if c >= UNSORTED:
                     sort_chunk("pred", c)

@@ -31,6 +31,7 @@ CHUNKS = TILES // CHUNK_TILES
 HEAD_CHUNKS = 6
 ROUND_CHUNKS = 2
 X_LAG = 3
+LAST_PARTS = (2, 2)
 LOAD_AHEAD = 3
 UNSORTED = 2
 
@@ -249,7 +250,7 @@ def tile_pecircuits_pa_t_kernel(
                     start=(g == 0),
                     stop=(g == D_PASSES - 1),
                 )
-            fed = som_pool.tile([P, CELLS], F32)
+            fed = som_pool.tile([P, CELLS], F32, tag="fed")
             nc.scalar.activation(out=fed[:], in_=feed[:], func=RELU)
             som_ff[(c, t)] = fed
 
@@ -264,7 +265,7 @@ def tile_pecircuits_pa_t_kernel(
                 start=True,
                 stop=True,
             )
-            result = out_pool.tile([P, CELLS], F32)
+            result = out_pool.tile([P, CELLS], F32, tag="result")
             nc.vector.tensor_tensor(
                 out=result[:], in0=som_ff[(c, t)][:], in1=inhibition[:], op=SUBTRACT
             )
@@ -272,6 +273,53 @@ def tile_pecircuits_pa_t_kernel(
                 out=result[:], in0=result[:], scalar1=float("inf"), scalar2=0.0, op0=MIN, op1=MAX
             )
             nc.sync.dma_start(out=out_chunks[c][:, t * CELLS : (t + 1) * CELLS], in_=result[:])
+
+        def last_chunk(c):
+            inhibited = {}
+            for t in range(CHUNK_TILES):
+                inhibition = psum.tile([P, BANK], F32, tag="bank")
+                mx(
+                    inhibition[:],
+                    quantised[("vip", c)],
+                    slice(t * P, (t + 1) * P),
+                    vs_q,
+                    slice(0, CELLS),
+                    start=True,
+                    stop=True,
+                )
+                copied = som_pool.tile([P, CELLS], F32, tag="fed")
+                nc.scalar.copy(out=copied[:], in_=inhibition[:])
+                inhibited[t] = copied
+            for t in range(CHUNK_TILES):
+                result = out_pool.tile([P, CELLS], F32, tag="result")
+                parts = LAST_PARTS[t]
+                width = CELLS // parts
+                for part in range(parts):
+                    cols = slice(part * width, (part + 1) * width)
+                    feed = psum.tile([P, BANK], F32, tag="bank")
+                    for g in range(D_PASSES):
+                        mx(
+                            feed[:, :width],
+                            quantised[("x", c)],
+                            slice((t * D_PASSES + g) * P, (t * D_PASSES + g + 1) * P),
+                            som_q,
+                            slice(g * CELLS + cols.start, g * CELLS + cols.stop),
+                            start=(g == 0),
+                            stop=(g == D_PASSES - 1),
+                        )
+                    nc.vector.scalar_tensor_tensor(
+                        out=result[:, cols],
+                        in0=feed[:, :width],
+                        scalar=0.0,
+                        in1=inhibited[t][:, cols],
+                        op0=MAX,
+                        op1=SUBTRACT,
+                    )
+                    nc.scalar.activation(out=result[:, cols], in_=result[:, cols], func=RELU)
+                    nc.sync.dma_start(
+                        out=out_chunks[c][:, t * CELLS + cols.start : t * CELLS + cols.stop],
+                        in_=result[:, cols],
+                    )
 
         units = [[c] for c in range(HEAD_CHUNKS)]
         units += [
@@ -323,6 +371,9 @@ def tile_pecircuits_pa_t_kernel(
             for c in unit(r - 1):
                 quantise_chunk("vip", c)
             for c in unit(r - X_LAG - 1):
+                if c == CHUNKS - 1:
+                    last_chunk(c)
+                    continue
                 for t in range(CHUNK_TILES):
                     feed_matmul(c, t)
                 for t in range(CHUNK_TILES):

@@ -28,12 +28,10 @@ BLOCKS = BANK // P
 TILES = BATCH // P
 CHUNK_TILES = 2
 CHUNKS = TILES // CHUNK_TILES
-HEAD_CHUNKS = 6
-ROUND_CHUNKS = 2
 X_LAG = 3
-LAST_PARTS = (2, 2)
-LOAD_AHEAD = 3
+LOAD_AHEAD = 4
 UNSORTED = 2
+LAST_PARTS = 2
 
 
 def tile_pecircuits_pa_t_kernel(
@@ -47,17 +45,11 @@ def tile_pecircuits_pa_t_kernel(
 
     with ExitStack() as stack:
         const = stack.enter_context(tc.tile_pool(name="const", bufs=1))
-        raw_pool = stack.enter_context(
-            tc.tile_pool(name="raw", bufs=(LOAD_AHEAD + 1) * ROUND_CHUNKS - 1)
-        )
-        sorted_pool = stack.enter_context(tc.tile_pool(name="sorted", bufs=2 * ROUND_CHUNKS))
-        grouped_pool = stack.enter_context(
-            tc.tile_pool(name="grouped", bufs=3 * ROUND_CHUNKS)
-        )
-        codes_pool = stack.enter_context(tc.tile_pool(name="codes", bufs=3 * ROUND_CHUNKS))
-        vip_pool = stack.enter_context(
-            tc.tile_pool(name="vip", bufs=(X_LAG + 2) * ROUND_CHUNKS)
-        )
+        raw_pool = stack.enter_context(tc.tile_pool(name="raw", bufs=LOAD_AHEAD + 2))
+        sorted_pool = stack.enter_context(tc.tile_pool(name="sorted", bufs=3))
+        grouped_pool = stack.enter_context(tc.tile_pool(name="grouped", bufs=5))
+        codes_pool = stack.enter_context(tc.tile_pool(name="codes", bufs=4))
+        vip_pool = stack.enter_context(tc.tile_pool(name="vip", bufs=X_LAG + 3))
         som_pool = stack.enter_context(tc.tile_pool(name="som", bufs=4))
         out_pool = stack.enter_context(tc.tile_pool(name="result", bufs=6))
         psum = stack.enter_context(tc.psum_pool(name="psum", bufs=8))
@@ -139,35 +131,55 @@ def tile_pecircuits_pa_t_kernel(
                 cols = slice(h * 2 * D_PASSES * P, (h + 1) * 2 * D_PASSES * P)
                 quantise(pairs[h][:], td_q[0][:, cols], td_q[1][:, cols])
 
-        def load_som_and_vs():
-            nc.sync.dma_start(
-                out=som_raw[:].rearrange("q (r k) -> q r k", r=BLOCKS),
-                in_=W_som_in.rearrange("(r q) k -> q r k", q=P),
-            )
-            nc.sync.dma_start(
-                out=vs_raw[:].rearrange("q (r k) -> q r k", r=BLOCKS),
-                in_=W_vip_som.rearrange("(r q) k -> q r k", q=P),
-            )
+        SOM_STEPS = 2
+        som_tiles = BLOCKS // SOM_STEPS
+        steps = range(SOM_STEPS + 1)
 
-        def prepare_som_and_vs():
-            som_words = som_grouped[:].bitcast(F32).rearrange(
-                "p (g r q u) -> p r g q u", g=D_PASSES, r=BLOCKS, u=2
-            )
-            for r in range(BLOCKS):
-                flip(
-                    every_second(som_raw[:].bitcast(F32)[:, r * BANK : (r + 1) * BANK]),
-                    som_words[:, r],
-                    either_copy(r),
+        def load_weights(step):
+            if step < SOM_STEPS:
+                first = step * som_tiles
+                nc.sync.dma_start(
+                    out=som_raw[:, first * D_IN : (first + som_tiles) * D_IN].rearrange(
+                        "q (r k) -> q r k", r=som_tiles
+                    ),
+                    in_=W_som_in.rearrange("(r q) k -> q r k", q=P)[:, first : first + som_tiles],
                 )
-            for h in range(2):
-                half = slice(h * BANK, (h + 1) * BANK)
-                flip(
-                    every_second(vs_raw[:].bitcast(F32)[:, half]),
-                    as_pairs(vs_grouped[:].bitcast(F32)[:, half]),
-                    either_copy(h),
+            else:
+                nc.sync.dma_start(
+                    out=vs_raw[:].rearrange("q (r k) -> q r k", r=BLOCKS),
+                    in_=W_vip_som.rearrange("(r q) k -> q r k", q=P),
                 )
-            quantise(som_grouped[:], som_q[0][:], som_q[1][:])
-            quantise(vs_grouped[:], vs_q[0][:], vs_q[1][:])
+
+        def flip_weights(step):
+            if step < SOM_STEPS:
+                som_words = som_grouped[:].bitcast(F32).rearrange(
+                    "p (g r q u) -> p r g q u", g=D_PASSES, r=BLOCKS, u=2
+                )
+                for r in range(step * som_tiles, (step + 1) * som_tiles):
+                    flip(
+                        every_second(som_raw[:].bitcast(F32)[:, r * BANK : (r + 1) * BANK]),
+                        som_words[:, r],
+                        either_copy(r),
+                    )
+            else:
+                for h in range(2):
+                    half = slice(h * BANK, (h + 1) * BANK)
+                    flip(
+                        every_second(vs_raw[:].bitcast(F32)[:, half]),
+                        as_pairs(vs_grouped[:].bitcast(F32)[:, half]),
+                        either_copy(h),
+                    )
+
+        def quantise_weights(step):
+            if step < SOM_STEPS:
+                width = som_tiles * P
+                for g in range(D_PASSES):
+                    first = g * CELLS + step * width
+                    cols = slice(first, first + width)
+                    values = slice(PACK * first, PACK * (first + width))
+                    quantise(som_grouped[:, values], som_q[0][:, cols], som_q[1][:, cols])
+            else:
+                quantise(vs_grouped[:], vs_q[0][:], vs_q[1][:])
 
         raw = {}
         sorted_words = {}
@@ -292,9 +304,8 @@ def tile_pecircuits_pa_t_kernel(
                 inhibited[t] = copied
             for t in range(CHUNK_TILES):
                 result = out_pool.tile([P, CELLS], F32, tag="result")
-                parts = LAST_PARTS[t]
-                width = CELLS // parts
-                for part in range(parts):
+                width = CELLS // LAST_PARTS
+                for part in range(LAST_PARTS):
                     cols = slice(part * width, (part + 1) * width)
                     feed = psum.tile([P, BANK], F32, tag="bank")
                     for g in range(D_PASSES):
@@ -321,21 +332,16 @@ def tile_pecircuits_pa_t_kernel(
                         in_=result[:, cols],
                     )
 
-        units = [[c] for c in range(HEAD_CHUNKS)]
-        units += [
-            list(range(c, c + ROUND_CHUNKS)) for c in range(HEAD_CHUNKS, CHUNKS, ROUND_CHUNKS)
-        ]
-
-        def unit(u):
-            return units[u] if 0 <= u < len(units) else []
+        def some(c):
+            return [c] if 0 <= c < CHUNKS else []
 
         def loads_for_round(r):
-            for c in unit(r):
+            for c in some(r):
                 load("pred", c)
-            for c in unit(r - X_LAG):
+            for c in some(r - X_LAG):
                 load("x", c)
-            if r == X_LAG:
-                load_som_and_vs()
+            if r - 1 in steps:
+                load_weights(r - 1)
 
         loads_for_round(0)
         load_td()
@@ -345,36 +351,35 @@ def tile_pecircuits_pa_t_kernel(
         quantise_chunk("pred", 0)
         prepare_td()
 
-        for r in range(len(units) + X_LAG + 1):
+        for r in range(CHUNKS + X_LAG + 1):
             loads_for_round(r + LOAD_AHEAD)
 
-            fresh = unit(r) if r > 0 else []
+            fresh = some(r) if r > 0 else []
             for c in fresh:
-                first = nc.vector.tensor_copy if c == fresh[0] else nc.scalar.copy
-                flip_chunk("pred", c, [first, nc.scalar.copy])
-            for c in unit(r + 1):
+                flip_chunk("pred", c, [nc.scalar.copy] * CHUNK_TILES)
+            for c in some(r + 1):
                 if c >= UNSORTED:
                     sort_chunk("pred", c)
-            for c in unit(r - X_LAG):
+            for c in some(r - X_LAG):
                 flip_chunk("x", c, [nc.scalar.copy] * CHUNK_TILES)
             for c in fresh:
                 quantise_chunk("pred", c)
-            for c in unit(r - X_LAG + 1):
+            for c in some(r - X_LAG + 1):
                 sort_chunk("x", c)
-            for c in unit(r - X_LAG):
+            for c in some(r - X_LAG):
                 quantise_chunk("x", c)
-            if r == X_LAG:
-                prepare_som_and_vs()
+            if r - 1 in steps:
+                flip_weights(r - 1)
+                quantise_weights(r - 1)
 
-            for c in unit(r - 1):
-                vip_matmuls(c)
-            for c in unit(r - 1):
-                quantise_chunk("vip", c)
-            for c in unit(r - X_LAG - 1):
+            for c in some(r - X_LAG - 1):
                 if c == CHUNKS - 1:
                     last_chunk(c)
-                    continue
-                for t in range(CHUNK_TILES):
-                    feed_matmul(c, t)
-                for t in range(CHUNK_TILES):
-                    inhibit(c, t)
+                else:
+                    for t in range(CHUNK_TILES):
+                        feed_matmul(c, t)
+                    for t in range(CHUNK_TILES):
+                        inhibit(c, t)
+            for c in some(r - 1):
+                vip_matmuls(c)
+                quantise_chunk("vip", c)

from contextlib import ExitStack

import concourse.mybir as mybir
from concourse.masks import make_identity

F32 = mybir.dt.float32
BF16 = mybir.dt.bfloat16
U32 = mybir.dt.uint32
U8 = mybir.dt.uint8
FP8X4 = mybir.dt.float8_e4m3fn_x4
RELU = mybir.ActivationFunctionType.Relu
SUBTRACT = mybir.AluOpType.subtract
MIN = mybir.AluOpType.min
MAX = mybir.AluOpType.max

BATCH = 4096
D_IN = 1024
CELLS = 512
FLOPS = 2 * BATCH * CELLS * (2 * D_IN + CELLS)

P = 128
PACK = 4
K_PASS = P * PACK
D_PASSES = D_IN // K_PASS
BANK = 512
BLOCKS = BANK // P

TILES = BATCH // P
CHUNK_TILES = 2
CHUNKS = TILES // CHUNK_TILES
X_LAG = 3
LOAD_AHEAD = 4
UNSORTED = 2
LAST_PARTS = 2


def tile_pecircuits_pa_t_kernel(
    tc, x_batch, predicted, W_vip_td, W_som_in, W_vip_som, out
):
    nc = tc.nc

    pred_chunks = predicted.rearrange("(c p t) k -> c p (t k)", p=P, t=CHUNK_TILES)
    x_chunks = x_batch.rearrange("(c p t) k -> c p (t k)", p=P, t=CHUNK_TILES)
    out_chunks = out.rearrange("(c p t) n -> c p (t n)", p=P, t=CHUNK_TILES)

    with ExitStack() as stack:
        const = stack.enter_context(tc.tile_pool(name="const", bufs=1))
        raw_pool = stack.enter_context(tc.tile_pool(name="raw", bufs=LOAD_AHEAD + 2))
        sorted_pool = stack.enter_context(tc.tile_pool(name="sorted", bufs=3))
        grouped_pool = stack.enter_context(tc.tile_pool(name="grouped", bufs=5))
        codes_pool = stack.enter_context(tc.tile_pool(name="codes", bufs=4))
        vip_pool = stack.enter_context(tc.tile_pool(name="vip", bufs=X_LAG + 3))
        som_pool = stack.enter_context(tc.tile_pool(name="som", bufs=4))
        out_pool = stack.enter_context(tc.tile_pool(name="result", bufs=6))
        psum = stack.enter_context(tc.psum_pool(name="psum", bufs=8))
        stack.enter_context(tc.manual_schedule())

        ident = const.tile([P, P], F32)
        make_identity(nc, ident[:])

        def as_pairs(words):
            return words.rearrange("p (g b u) -> p g b u", g=D_PASSES, u=2)

        def every_second(words):
            return [
                words[:, 2 * g * P + u : 2 * (g + 1) * P : 2] for g in range(D_PASSES) for u in range(2)
            ]

        def flip(blocks, dest, copy_out):
            bank = psum.tile([P, BANK], F32, tag="bank")
            for c in range(BLOCKS):
                nc.tensor.transpose(bank[:, c * P : (c + 1) * P], blocks[c], ident[:])
            copy_out(out=dest, in_=bank[:].rearrange("p (g u b) -> p g b u", g=D_PASSES, u=2))

        def quantise(grouped, codes, scales):
            nc.vector.quantize_mx(out=codes.bitcast(FP8X4), scales=scales, in_=grouped)

        def mx(acc, stationary, s_cols, moving, m_cols, start, stop):
            nc.tensor.matmul_mx(
                out=acc,
                lhsT=stationary[0][:, s_cols].bitcast(FP8X4),
                lhsT_scale=stationary[1][:, s_cols],
                rhs=moving[0][:, m_cols].bitcast(FP8X4),
                rhs_scale=moving[1][:, m_cols],
                start=start,
                stop=stop,
            )

        td_raw = const.tile([P, PACK * D_IN], BF16)
        td_q = (
            const.tile([P, PACK * D_PASSES * P], U32, name="td_codes", align_bytes=64),
            const.tile([P, PACK * D_PASSES * P], U8, name="td_scales", align_bytes=64),
        )
        som_raw = const.tile([P, BLOCKS * D_IN], BF16)
        som_grouped = const.tile([P, D_PASSES * CELLS * PACK], BF16, align_bytes=64)
        som_q = (
            const.tile([P, D_PASSES * CELLS], U32, name="som_codes", align_bytes=64),
            const.tile([P, D_PASSES * CELLS], U8, name="som_scales", align_bytes=64),
        )
        vs_raw = const.tile([P, BLOCKS * CELLS], BF16)
        vs_grouped = const.tile([P, CELLS * PACK], BF16, align_bytes=64)
        vs_q = (
            const.tile([P, CELLS], U32, name="vs_codes", align_bytes=64),
            const.tile([P, CELLS], U8, name="vs_scales", align_bytes=64),
        )

        def either_copy(n):
            return nc.scalar.copy if n % 2 == 0 else nc.vector.tensor_copy

        def load_td():
            rows = W_vip_td.rearrange("(q j) k -> q (j k)", j=PACK)
            for j in range(PACK):
                row = slice(j * D_IN, (j + 1) * D_IN)
                nc.sync.dma_start(out=td_raw[:, row], in_=rows[:, row])

        def prepare_td():
            pairs = []
            for h in range(2):
                grouped = grouped_pool.tile(
                    [P, CHUNK_TILES * D_IN], BF16, tag="grouped_chunk", align_bytes=64
                )
                for t in range(2):
                    j = 2 * h + t
                    flip(
                        every_second(td_raw[:].bitcast(F32)[:, j * BANK : (j + 1) * BANK]),
                        as_pairs(grouped[:].bitcast(F32)[:, t * BANK : (t + 1) * BANK]),
                        either_copy(t),
                    )
                pairs.append(grouped)
            for h in range(2):
                cols = slice(h * 2 * D_PASSES * P, (h + 1) * 2 * D_PASSES * P)
                quantise(pairs[h][:], td_q[0][:, cols], td_q[1][:, cols])

        SOM_STEPS = 2
        som_tiles = BLOCKS // SOM_STEPS
        steps = range(SOM_STEPS + 1)

        def load_weights(step):
            if step < SOM_STEPS:
                first = step * som_tiles
                nc.sync.dma_start(
                    out=som_raw[:, first * D_IN : (first + som_tiles) * D_IN].rearrange(
                        "q (r k) -> q r k", r=som_tiles
                    ),
                    in_=W_som_in.rearrange("(r q) k -> q r k", q=P)[:, first : first + som_tiles],
                )
            else:
                nc.sync.dma_start(
                    out=vs_raw[:].rearrange("q (r k) -> q r k", r=BLOCKS),
                    in_=W_vip_som.rearrange("(r q) k -> q r k", q=P),
                )

        def flip_weights(step):
            if step < SOM_STEPS:
                som_words = som_grouped[:].bitcast(F32).rearrange(
                    "p (g r q u) -> p r g q u", g=D_PASSES, r=BLOCKS, u=2
                )
                for r in range(step * som_tiles, (step + 1) * som_tiles):
                    flip(
                        every_second(som_raw[:].bitcast(F32)[:, r * BANK : (r + 1) * BANK]),
                        som_words[:, r],
                        either_copy(r),
                    )
            else:
                for h in range(2):
                    half = slice(h * BANK, (h + 1) * BANK)
                    flip(
                        every_second(vs_raw[:].bitcast(F32)[:, half]),
                        as_pairs(vs_grouped[:].bitcast(F32)[:, half]),
                        either_copy(h),
                    )

        def quantise_weights(step):
            if step < SOM_STEPS:
                width = som_tiles * P
                for g in range(D_PASSES):
                    first = g * CELLS + step * width
                    cols = slice(first, first + width)
                    values = slice(PACK * first, PACK * (first + width))
                    quantise(som_grouped[:, values], som_q[0][:, cols], som_q[1][:, cols])
            else:
                quantise(vs_grouped[:], vs_q[0][:], vs_q[1][:])

        raw = {}
        sorted_words = {}
        grouped_of = {}
        quantised = {}
        source = {"pred": pred_chunks, "x": x_chunks}

        def load(name, c):
            rows = raw_pool.tile([P, CHUNK_TILES * D_IN], BF16, tag=name + "_raw")
            nc.sync.dma_start(out=rows[:], in_=source[name][c])
            raw[(name, c)] = rows

        def sort_chunk(name, c):
            words = sorted_pool.tile([P, CHUNK_TILES * BANK], F32, tag=name + "_sorted")
            nc.vector.tensor_copy(
                out=words[:].rearrange("p (u w) -> p u w", u=2),
                in_=raw[(name, c)][:].bitcast(F32).rearrange("p (w u) -> p u w", u=2),
            )
            sorted_words[(name, c)] = words

        def flip_chunk(name, c, copies):
            grouped = grouped_pool.tile(
                [P, CHUNK_TILES * D_IN], BF16, tag="grouped_chunk", align_bytes=64
            )
            if (name, c) in sorted_words:
                halves = sorted_words[(name, c)][:].rearrange("p (u w) -> p u w", u=2)
            else:
                halves = raw[(name, c)][:].bitcast(F32).rearrange("p (w u) -> p u w", u=2)
            for t in range(CHUNK_TILES):
                starts = [(t * D_PASSES + g) * P for g in range(D_PASSES)]
                flip(
                    [halves[:, u, w : w + P] for w in starts for u in range(2)],
                    as_pairs(grouped[:].bitcast(F32)[:, t * BANK : (t + 1) * BANK]),
                    copies[t],
                )
            grouped_of[(name, c)] = grouped

        def quantise_chunk(name, c):
            grouped = grouped_of[(name, c)]
            width = grouped.shape[1] // PACK
            pool = vip_pool if name == "vip" else codes_pool
            codes = pool.tile([P, width], U32, tag=name + "_codes", align_bytes=64)
            scales = pool.tile([P, width], U8, tag=name + "_scales", align_bytes=64)
            quantise(grouped[:], codes[:], scales[:])
            quantised[(name, c)] = (codes, scales)

        def vip_matmuls(c):
            vip = grouped_pool.tile([P, CHUNK_TILES * BANK], BF16, tag="vip", align_bytes=64)
            for t in range(CHUNK_TILES):
                bank = psum.tile([P, BANK], F32, tag="bank")
                for j in range(PACK):
                    for g in range(D_PASSES):
                        mx(
                            bank[:, j * P : (j + 1) * P],
                            td_q,
                            slice((j * D_PASSES + g) * P, (j * D_PASSES + g + 1) * P),
                            quantised[("pred", c)],
                            slice((t * D_PASSES + g) * P, (t * D_PASSES + g + 1) * P),
                            start=(g == 0),
                            stop=(g == D_PASSES - 1),
                        )
                nc.scalar.activation(
                    out=vip[:, t * BANK : (t + 1) * BANK].rearrange("p (b j) -> p b j", j=PACK),
                    in_=bank[:].rearrange("p (j b) -> p b j", j=PACK),
                    func=RELU,
                )
            grouped_of[("vip", c)] = vip

        som_ff = {}

        def feed_matmul(c, t):
            feed = psum.tile([P, BANK], F32, tag="bank")
            for g in range(D_PASSES):
                mx(
                    feed[:],
                    quantised[("x", c)],
                    slice((t * D_PASSES + g) * P, (t * D_PASSES + g + 1) * P),
                    som_q,
                    slice(g * CELLS, (g + 1) * CELLS),
                    start=(g == 0),
                    stop=(g == D_PASSES - 1),
                )
            fed = som_pool.tile([P, CELLS], F32, tag="fed")
            nc.scalar.activation(out=fed[:], in_=feed[:], func=RELU)
            som_ff[(c, t)] = fed

        def inhibit(c, t):
            inhibition = psum.tile([P, BANK], F32, tag="bank")
            mx(
                inhibition[:],
                quantised[("vip", c)],
                slice(t * P, (t + 1) * P),
                vs_q,
                slice(0, CELLS),
                start=True,
                stop=True,
            )
            result = out_pool.tile([P, CELLS], F32, tag="result")
            nc.vector.tensor_tensor(
                out=result[:], in0=som_ff[(c, t)][:], in1=inhibition[:], op=SUBTRACT
            )
            nc.gpsimd.tensor_scalar(
                out=result[:], in0=result[:], scalar1=float("inf"), scalar2=0.0, op0=MIN, op1=MAX
            )
            nc.sync.dma_start(out=out_chunks[c][:, t * CELLS : (t + 1) * CELLS], in_=result[:])

        def last_chunk(c):
            inhibited = {}
            for t in range(CHUNK_TILES):
                inhibition = psum.tile([P, BANK], F32, tag="bank")
                mx(
                    inhibition[:],
                    quantised[("vip", c)],
                    slice(t * P, (t + 1) * P),
                    vs_q,
                    slice(0, CELLS),
                    start=True,
                    stop=True,
                )
                copied = som_pool.tile([P, CELLS], F32, tag="fed")
                nc.scalar.copy(out=copied[:], in_=inhibition[:])
                inhibited[t] = copied
            for t in range(CHUNK_TILES):
                result = out_pool.tile([P, CELLS], F32, tag="result")
                width = CELLS // LAST_PARTS
                for part in range(LAST_PARTS):
                    cols = slice(part * width, (part + 1) * width)
                    feed = psum.tile([P, BANK], F32, tag="bank")
                    for g in range(D_PASSES):
                        mx(
                            feed[:, :width],
                            quantised[("x", c)],
                            slice((t * D_PASSES + g) * P, (t * D_PASSES + g + 1) * P),
                            som_q,
                            slice(g * CELLS + cols.start, g * CELLS + cols.stop),
                            start=(g == 0),
                            stop=(g == D_PASSES - 1),
                        )
                    nc.vector.scalar_tensor_tensor(
                        out=result[:, cols],
                        in0=feed[:, :width],
                        scalar=0.0,
                        in1=inhibited[t][:, cols],
                        op0=MAX,
                        op1=SUBTRACT,
                    )
                    nc.scalar.activation(out=result[:, cols], in_=result[:, cols], func=RELU)
                    nc.sync.dma_start(
                        out=out_chunks[c][:, t * CELLS + cols.start : t * CELLS + cols.stop],
                        in_=result[:, cols],
                    )

        def some(c):
            return [c] if 0 <= c < CHUNKS else []

        def loads_for_round(r):
            for c in some(r):
                load("pred", c)
            for c in some(r - X_LAG):
                load("x", c)
            if r - 1 in steps:
                load_weights(r - 1)

        loads_for_round(0)
        load_td()
        for r in range(1, LOAD_AHEAD):
            loads_for_round(r)
        flip_chunk("pred", 0, [nc.scalar.copy] * CHUNK_TILES)
        quantise_chunk("pred", 0)
        prepare_td()

        for r in range(CHUNKS + X_LAG + 1):
            loads_for_round(r + LOAD_AHEAD)

            fresh = some(r) if r > 0 else []
            for c in fresh:
                flip_chunk("pred", c, [nc.scalar.copy] * CHUNK_TILES)
            for c in some(r + 1):
                if c >= UNSORTED:
                    sort_chunk("pred", c)
            for c in some(r - X_LAG):
                flip_chunk("x", c, [nc.scalar.copy] * CHUNK_TILES)
            for c in fresh:
                quantise_chunk("pred", c)
            for c in some(r - X_LAG + 1):
                sort_chunk("x", c)
            for c in some(r - X_LAG):
                quantise_chunk("x", c)
            if r - 1 in steps:
                flip_weights(r - 1)
                quantise_weights(r - 1)

            for c in some(r - X_LAG - 1):
                if c == CHUNKS - 1:
                    last_chunk(c)
                else:
                    for t in range(CHUNK_TILES):
                        feed_matmul(c, t)
                    for t in range(CHUNK_TILES):
                        inhibit(c, t)
            for c in some(r - 1):
                vip_matmuls(c)
                quantise_chunk("vip", c)
